import numpy as np
import ml_dtypes


BF16 = ml_dtypes.bfloat16


def bf(x):
    return np.asarray(x, np.float32).astype(BF16)


def f64(x):
    return np.asarray(x).astype(np.float64)


E2M1 = np.array([0.0, 0.5, 1.0, 1.5, 2.0, 3.0, 4.0, 6.0, -0.0, -0.5, -1.0, -1.5, -2.0, -3.0, -4.0, -6.0])


def pack_weight(w, fmt):
    k, n = w.shape
    w = f64(bf(w)).reshape(k // 32, 32, n)
    amax = np.abs(w).max(1)
    if fmt == "e4m3":
        byte = np.frexp(amax)[1] - 1 + 127 - 7
    else:
        mant, ex = np.frexp(amax / 6.0)
        byte = np.where(mant > 0.5, ex, ex - 1) + 127
    byte = np.clip(np.where(amax > 0, byte, 1), 1, 254)
    scaled = (w * np.exp2(127.0 - byte)[:, None, :]).reshape(k, n).astype(np.float32)
    by_word = np.ascontiguousarray(scaled.reshape(k // 512, 128, 4, n).transpose(0, 1, 3, 2))
    if fmt == "e4m3":
        words = by_word.astype(ml_dtypes.float8_e4m3fn).view(np.uint8)
    else:
        c = by_word.astype(ml_dtypes.float4_e2m1fn).view(np.uint8) & 0xF
        words = c[..., 0::2] | (c[..., 1::2] << 4)
    return np.ascontiguousarray(words), np.ascontiguousarray(byte.astype(np.uint8).reshape(k // 512, 16, n))


def unpack_weight(words, scales, fmt):
    g, p, n, _ = words.shape
    if fmt == "e4m3":
        vals = np.ascontiguousarray(words).view(ml_dtypes.float8_e4m3fn).astype(np.float64)
    else:
        nib = np.empty((g, p, n, 4), np.uint8)
        nib[..., 0::2] = words & 0xF
        nib[..., 1::2] = words >> 4
        vals = E2M1[nib]
    vals = vals * np.repeat(np.exp2(scales.astype(np.float64) - 127.0), 8, axis=1)[..., None]
    return vals.transpose(0, 1, 3, 2).reshape(g * 512, n)

def pack4(w):
    words, scales = pack_weight(w, "e2m1")
    return words.reshape(words.shape[0], 128, -1), scales


def unpack4(words, scales):
    return unpack_weight(words.reshape(words.shape[0], 128, -1, 2), scales, "e2m1")


def kspread(k):
    return np.exp2(np.repeat(np.random.randint(-6, 7, k // 32), 32).astype(np.float64))


B, S, H, NH, HD, ROT = 2, 768, 2048, 8, 256, 32
BASE = 10000.0


def rotate_half(x):
    half = x.shape[-1] // 2
    return np.concatenate((-x[..., half:], x[..., :half]), axis=-1)


def rope_tables(seq_len):
    inv_freq = 1.0 / (BASE ** (np.arange(0, ROT, 2) / ROT))
    freqs = np.arange(seq_len)[:, None] * inv_freq[None, :]
    emb = np.concatenate((freqs, freqs), axis=-1)
    return np.cos(emb), np.sin(emb)


def setup_inputs():
    s = kspread(H)
    hidden_states = np.random.standard_normal((B, S, H)) * s
    hidden_states_words, hidden_states_scales = pack4(hidden_states.reshape(B * S, H).T)
    words, scales = pack4(np.random.standard_normal((H, 3 * H)) / np.sqrt(H) / s[:, None])
    b_qkv = bf(np.random.standard_normal(3 * H) * 0.3)
    return {"hidden_states_words": hidden_states_words,
            "hidden_states_scales": hidden_states_scales,
            "W_qkv_words": words,
            "W_qkv_scales": scales,
            "b_qkv": b_qkv}


def reference(hidden_states_words, hidden_states_scales, W_qkv_words, W_qkv_scales, b_qkv):
    qkv = (unpack4(hidden_states_words, hidden_states_scales).T.reshape(B, S, H) @ unpack4(W_qkv_words, W_qkv_scales)) + f64(b_qkv)
    qkv = qkv.reshape(B, S, NH, 3 * HD)
    q = qkv[..., :HD].transpose(0, 2, 1, 3)
    k = qkv[..., HD:2 * HD].transpose(0, 2, 1, 3)
    v = qkv[..., 2 * HD:].transpose(0, 2, 1, 3)
    cos, sin = rope_tables(S)
    q_rot, q_pass = q[..., :ROT], q[..., ROT:]
    k_rot, k_pass = k[..., :ROT], k[..., ROT:]
    q_rot = q_rot * cos + rotate_half(q_rot) * sin
    k_rot = k_rot * cos + rotate_half(k_rot) * sin
    q = np.concatenate((q_rot, q_pass), axis=-1)
    k = np.concatenate((k_rot, k_pass), axis=-1)
    return q, k, np.ascontiguousarray(v)

@@ -1,0 +1,258 @@
+import math
+from contextlib import ExitStack
+
+import concourse.mybir as mybir
+
+F32 = mybir.dt.float32
+BF16 = mybir.dt.bfloat16
+I32 = mybir.dt.int32
+U8 = mybir.dt.uint8
+FP4X4 = mybir.dt.float4_e2m1fn_x4
+ALU = mybir.AluOpType
+ACT = mybir.ActivationFunctionType
+
+BATCH, SEQ, HIDDEN, HEADS, HEAD_DIM, ROT = 2, 768, 2048, 8, 256, 32
+BASE = 10000.0
+P = 128
+PASSES = HIDDEN // 512
+N_TILE = 512
+COL_BLOCKS = 3 * HIDDEN // N_TILE
+SEQ_TILES = SEQ // P
+TOKEN_TILES = BATCH * SEQ_TILES
+HALF = ROT // 2
+X_CODE_CHUNKS = ((0, 3), (3, 6), (6, 12))
+X_PLANE_CHUNKS = ((0, 3), (3, 12))
+HEAD_TILES = 3
+WARM_UP = 10
+SIN_LIMIT = 0.5 - 1e-6
+
+FLOPS = 2 * BATCH * SEQ * HIDDEN * 3 * HIDDEN
+
+
+def load_scale_rows(nc, plane, scales, cols):
+    for quad in range(4):
+        nc.sync.dma_start(
+            out=plane[32 * quad : 32 * quad + 4, :, :].bitcast(I32),
+            in_=scales[:, 4 * quad : 4 * quad + 4, cols].rearrange("g r n -> r g n").bitcast(I32),
+        )
+
+
+def load_codes(nc, codes, words, passes, byte_cols):
+    nc.sync.dma_start(
+        out=codes[:].bitcast(I32),
+        in_=words[passes, :, byte_cols].rearrange("g p c -> p g c").bitcast(I32),
+    )
+
+
+def chunk_of(chunks, m):
+    for c, (m0, m1) in enumerate(chunks):
+        if m0 <= m < m1:
+            return c, m - m0
+    raise ValueError("no such token tile")
+
+
+def tile_pgtattention_pa_kernel(
+    tc, hidden_states_words, hidden_states_scales, W_qkv_words, W_qkv_scales, b_qkv, out_0, out_1, out_2
+):
+    nc = tc.nc
+    outs = (out_0, out_1, out_2)
+
+    with ExitStack() as ctx:
+        keep = ctx.enter_context(tc.tile_pool(name="keep", bufs=1))
+        stage_pool = ctx.enter_context(tc.tile_pool(name="stage", bufs=4))
+        rope_pool = ctx.enter_context(tc.tile_pool(name="rope", bufs=2))
+        psum = ctx.enter_context(tc.psum_pool(name="psum", bufs=8))
+        ctx.enter_context(tc.manual_schedule())
+
+        w_first = keep.tile([P, 1, 2 * N_TILE], U8, name="w_first", align_bytes=64)
+        w_rest = keep.tile([P, PASSES - 1, 2 * N_TILE], U8, name="w_rest", align_bytes=64)
+        w_codes = [None]
+        w_planes = []
+        bias = []
+        for n in range(COL_BLOCKS):
+            if n > 0:
+                w_codes.append(keep.tile([P, PASSES, 2 * N_TILE], U8, name="w_codes%d" % n, align_bytes=64))
+            w_planes.append(keep.tile([P, PASSES, N_TILE], U8, name="w_plane%d" % n, align_bytes=64))
+            bias.append(keep.tile([P, N_TILE], BF16, name="bias%d" % n))
+        x_codes = []
+        for c, (m0, m1) in enumerate(X_CODE_CHUNKS):
+            x_codes.append(keep.tile([P, PASSES, 2 * P * (m1 - m0)], U8, name="x_codes%d" % c, align_bytes=64))
+        x_planes = []
+        for c, (m0, m1) in enumerate(X_PLANE_CHUNKS):
+            x_planes.append(keep.tile([P, PASSES, P * (m1 - m0)], U8, name="x_plane%d" % c, align_bytes=64))
+
+        def w_cols(n):
+            return slice(N_TILE * n, N_TILE * (n + 1))
+
+        def w_byte_cols(n):
+            return slice(2 * N_TILE * n, 2 * N_TILE * (n + 1))
+
+        def load_bias(n):
+            nc.gpsimd.dma_start(out=bias[n][:], in_=b_qkv[w_cols(n)].partition_broadcast(P))
+
+        def load_w_block(n):
+            nc.vector.memset(w_planes[n][:].bitcast(I32), 0)
+            load_scale_rows(nc, w_planes[n], W_qkv_scales, w_cols(n))
+            load_codes(nc, w_codes[n], W_qkv_words, slice(0, PASSES), w_byte_cols(n))
+            load_bias(n)
+
+        def load_x_codes(c):
+            m0, m1 = X_CODE_CHUNKS[c]
+            load_codes(nc, x_codes[c], hidden_states_words, slice(0, PASSES), slice(2 * P * m0, 2 * P * m1))
+
+        def load_x_plane(c):
+            m0, m1 = X_PLANE_CHUNKS[c]
+            load_scale_rows(nc, x_planes[c], hidden_states_scales, slice(P * m0, P * m1))
+
+        idle = keep.tile([P, N_TILE], BF16, name="idle")
+        nc.vector.memset(idle[:], 0.0)
+        idle_acc = psum.tile([P, N_TILE], F32, name="acc")
+        for i in range(WARM_UP):
+            nc.tensor.matmul(out=idle_acc[:], lhsT=idle[:, 0:P], rhs=idle[:], start=True, stop=True)
+        nc.gpsimd.memset(w_planes[0][:].bitcast(F32), 0.0)
+        nc.gpsimd.memset(x_planes[0][:].bitcast(F32), 0.0)
+        nc.vector.memset(x_planes[1][:].bitcast(I32), 0)
+        load_codes(nc, w_first, W_qkv_words, slice(0, 1), w_byte_cols(0))
+        load_x_codes(0)
+        load_scale_rows(nc, w_planes[0], W_qkv_scales, w_cols(0))
+        load_x_plane(0)
+        load_codes(nc, w_rest, W_qkv_words, slice(1, PASSES), w_byte_cols(0))
+        load_x_plane(1)
+        load_x_codes(1)
+        load_x_codes(2)
+        pos_i = keep.tile([P, SEQ_TILES], I32, name="pos_i")
+        nc.gpsimd.iota(pos_i[:], pattern=[[P, SEQ_TILES]], base=0, channel_multiplier=1)
+        load_bias(0)
+
+        pos = keep.tile([P, SEQ_TILES], F32, name="pos")
+        nc.vector.tensor_copy(out=pos[:], in_=pos_i[:])
+        turns = keep.tile([P, SEQ_TILES, 2, HALF], F32, name="turns")
+        for i in range(HALF):
+            nc.vector.tensor_scalar(
+                out=turns[:, :, :, i],
+                in0=pos[:].unsqueeze(2).to_broadcast([P, SEQ_TILES, 2]),
+                scalar1=1.0 / (BASE ** (i / HALF)) / (2.0 * math.pi),
+                scalar2=None,
+                op0=ALU.mult,
+            )
+        nc.vector.tensor_scalar(
+            out=turns[:, :, 0, :], in0=turns[:, :, 0, :], scalar1=0.25, scalar2=None, op0=ALU.add
+        )
+        whole_i = keep.tile([P, SEQ_TILES, 2, HALF], I32, name="whole_i")
+        nc.vector.tensor_copy(out=whole_i[:], in_=turns[:])
+        whole = keep.tile([P, SEQ_TILES, 2, HALF], F32, name="whole")
+        nc.vector.tensor_copy(out=whole[:], in_=whole_i[:])
+        frac = keep.tile([P, SEQ_TILES, 2, HALF], F32, name="frac")
+        nc.vector.tensor_tensor(out=frac[:], in0=turns[:], in1=whole[:], op=ALU.subtract)
+        over = keep.tile([P, SEQ_TILES, 2, HALF], F32, name="over")
+        nc.vector.tensor_scalar(out=over[:], in0=frac[:], scalar1=0.5, scalar2=None, op0=ALU.is_gt)
+        wrapped = keep.tile([P, SEQ_TILES, 2, HALF], F32, name="wrapped")
+        nc.vector.tensor_tensor(out=wrapped[:], in0=frac[:], in1=over[:], op=ALU.subtract)
+        clamped = keep.tile([P, SEQ_TILES, 2, HALF], F32, name="clamped")
+        nc.vector.tensor_scalar(
+            out=clamped[:], in0=wrapped[:], scalar1=-SIN_LIMIT, scalar2=SIN_LIMIT, op0=ALU.max, op1=ALU.min
+        )
+        cos_sin = keep.tile([P, SEQ_TILES, 2, HALF], F32, name="cos_sin")
+        nc.scalar.activation(out=cos_sin[:], in_=clamped[:], func=ACT.Sin, scale=2.0 * math.pi)
+        cos_t = keep.tile([P, SEQ_TILES, 4, HALF], F32, name="cos_t")
+        nc.vector.tensor_copy(
+            out=cos_t[:], in_=cos_sin[:, :, 0, :].unsqueeze(2).to_broadcast([P, SEQ_TILES, 4, HALF])
+        )
+        sin_t = keep.tile([P, SEQ_TILES, 2, 2, HALF], F32, name="sin_t")
+        nc.vector.tensor_scalar(
+            out=sin_t[:, :, :, 0, :],
+            in0=cos_sin[:, :, 1, :].unsqueeze(2).to_broadcast([P, SEQ_TILES, 2, HALF]),
+            scalar1=-1.0,
+            scalar2=None,
+            op0=ALU.mult,
+        )
+        nc.vector.tensor_copy(
+            out=sin_t[:, :, :, 1, :],
+            in_=cos_sin[:, :, 1, :].unsqueeze(2).to_broadcast([P, SEQ_TILES, 2, HALF]),
+        )
+        cos_v = cos_t[:].rearrange("p j (s r) i -> p j s (r i)", s=2)
+        sin_v = sin_t[:]
+
+        def w_operand(n, g):
+            if n > 0:
+                return w_codes[n][:, g, :]
+            return w_first[:, 0, :] if g == 0 else w_rest[:, g - 1, :]
+
+        def group(n, b, j0, j1, s0, s1, order):
+            nj = j1 - j0
+            width = HEAD_DIM * (s1 - s0)
+            stage = stage_pool.tile([P, nj, width], F32, name="stage")
+            accs = {}
+            for j, g in order:
+                m = SEQ_TILES * b + j
+                if g == 0:
+                    acc = psum.tile([P, width], F32, name="acc")
+                    accs[j] = acc
+                cc, cm = chunk_of(X_CODE_CHUNKS, m)
+                pc, pm = chunk_of(X_PLANE_CHUNKS, m)
+                nc.tensor.matmul_mx(
+                    out=accs[j][:],
+                    lhsT=x_codes[cc][:, g, 2 * P * cm : 2 * P * (cm + 1)].bitcast(FP4X4),
+                    lhsT_scale=x_planes[pc][:, g, P * pm : P * (pm + 1)],
+                    rhs=w_operand(n, g)[:, 2 * HEAD_DIM * s0 : 2 * HEAD_DIM * s1].bitcast(FP4X4),
+                    rhs_scale=w_planes[n][:, g, HEAD_DIM * s0 : HEAD_DIM * s1],
+                    start=(g == 0),
+                    stop=(g == PASSES - 1),
+                )
+                if g == PASSES - 1:
+                    nc.vector.tensor_tensor(
+                        out=stage[:, j - j0, :],
+                        in0=accs[j][:],
+                        in1=bias[n][:, HEAD_DIM * s0 : HEAD_DIM * s1],
+                        op=ALU.add,
+                    )
+                    if n == 0 and m + 1 < COL_BLOCKS:
+                        load_w_block(m + 1)
+
+            pieces = [2 * n + s for s in range(s0, s1)]
+            rot = [k for k in range(s1 - s0) if pieces[k] % 3 != 2]
+            view = stage[:].rearrange("p j (s f) -> p j s f", f=HEAD_DIM)
+            if rot:
+                r0, r1 = rot[0], rot[-1] + 1
+                nr = r1 - r0
+                straight = rope_pool.tile([P, nj, nr, ROT], F32, name="straight")
+                crossed = rope_pool.tile([P, nj, nr, ROT], F32, name="crossed")
+                nc.vector.tensor_tensor(
+                    out=straight[:], in0=view[:, :, r0:r1, 0:ROT], in1=cos_v[:, j0:j1, 0:nr, :], op=ALU.mult
+                )
+                nc.vector.tensor_tensor(
+                    out=crossed[:, :, :, 0:HALF],
+                    in0=view[:, :, r0:r1, HALF:ROT],
+                    in1=sin_v[:, j0:j1, 0:nr, 0, :],
+                    op=ALU.mult,
+                )
+                nc.vector.tensor_tensor(
+                    out=crossed[:, :, :, HALF:ROT],
+                    in0=view[:, :, r0:r1, 0:HALF],
+                    in1=sin_v[:, j0:j1, 0:nr, 1, :],
+                    op=ALU.mult,
+                )
+                nc.vector.tensor_tensor(
+                    out=view[:, :, r0:r1, 0:ROT], in0=straight[:], in1=crossed[:], op=ALU.add
+                )
+            for k, q in enumerate(pieces):
+                dst = outs[q % 3][b, q // 3, P * j0 : P * j1, :]
+                nc.scalar.dma_start(out=dst.rearrange("(j p) f -> p j f", p=P), in_=view[:, :, k, :])
+
+        def tile_by_tile(j0, j1):
+            return [(j, g) for j in range(j0, j1) for g in range(PASSES)]
+
+        for n in range(COL_BLOCKS):
+            for b in range(BATCH):
+                if n == 0 and b == 0:
+                    order = [(j, 0) for j in range(HEAD_TILES)]
+                    order += [(j, g) for j in range(HEAD_TILES) for g in range(1, PASSES)]
+                    order += tile_by_tile(HEAD_TILES, SEQ_TILES)
+                    group(n, b, 0, SEQ_TILES, 0, 2, order)
+                elif n == COL_BLOCKS - 1:
+                    group(n, b, 0, SEQ_TILES, 0, 1, tile_by_tile(0, SEQ_TILES))
+                else:
+                    group(n, b, 0, SEQ_TILES, 0, 2, tile_by_tile(0, SEQ_TILES))
+        group(COL_BLOCKS - 1, 0, 0, SEQ_TILES, 1, 2, tile_by_tile(0, SEQ_TILES))
+        for j0, j1 in ((0, 3), (3, 5), (5, 6)):
+            group(COL_BLOCKS - 1, 1, j0, j1, 1, 2, tile_by_tile(j0, j1))

@@ -22,7 +22,7 @@ TOKEN_TILES = BATCH * SEQ_TILES
 HALF = ROT // 2
 X_CODE_CHUNKS = ((0, 3), (3, 6), (6, 12))
 X_PLANE_CHUNKS = ((0, 3), (3, 12))
-HEAD_TILES = 3
+UNIT = 3
 WARM_UP = 10
 SIN_LIMIT = 0.5 - 1e-6
 
@@ -59,9 +59,10 @@ def tile_pgtattention_pa_kernel(
 
     with ExitStack() as ctx:
         keep = ctx.enter_context(tc.tile_pool(name="keep", bufs=1))
-        stage_pool = ctx.enter_context(tc.tile_pool(name="stage", bufs=4))
+        stage_pool = ctx.enter_context(tc.tile_pool(name="stage", bufs=6))
         rope_pool = ctx.enter_context(tc.tile_pool(name="rope", bufs=2))
-        psum = ctx.enter_context(tc.psum_pool(name="psum", bufs=8))
+        psum = ctx.enter_context(tc.psum_pool(name="psum", bufs=2))
+        idle_psum = ctx.enter_context(tc.psum_pool(name="idle_psum", bufs=1))
         ctx.enter_context(tc.manual_schedule())
 
         w_first = keep.tile([P, 1, 2 * N_TILE], U8, name="w_first", align_bytes=64)
@@ -91,7 +92,7 @@ def tile_pgtattention_pa_kernel(
             nc.gpsimd.dma_start(out=bias[n][:], in_=b_qkv[w_cols(n)].partition_broadcast(P))
 
         def load_w_block(n):
-            nc.vector.memset(w_planes[n][:].bitcast(I32), 0)
+            nc.gpsimd.memset(w_planes[n][:].bitcast(F32), 0.0)
             load_scale_rows(nc, w_planes[n], W_qkv_scales, w_cols(n))
             load_codes(nc, w_codes[n], W_qkv_words, slice(0, PASSES), w_byte_cols(n))
             load_bias(n)
@@ -106,7 +107,7 @@ def tile_pgtattention_pa_kernel(
 
         idle = keep.tile([P, N_TILE], BF16, name="idle")
         nc.vector.memset(idle[:], 0.0)
-        idle_acc = psum.tile([P, N_TILE], F32, name="acc")
+        idle_acc = idle_psum.tile([P, N_TILE], F32, name="idle_acc")
         for i in range(WARM_UP):
             nc.tensor.matmul(out=idle_acc[:], lhsT=idle[:, 0:P], rhs=idle[:], start=True, stop=True)
         nc.gpsimd.memset(w_planes[0][:].bitcast(F32), 0.0)
@@ -178,20 +179,21 @@ def tile_pgtattention_pa_kernel(
                 return w_codes[n][:, g, :]
             return w_first[:, 0, :] if g == 0 else w_rest[:, g - 1, :]
 
-        def group(n, b, j0, j1, s0, s1, order):
-            nj = j1 - j0
+        blocks_loaded = [1]
+
+        def unit(n, b, j0, j1, s0, s1, stage, first_j, pass_zero_first):
             width = HEAD_DIM * (s1 - s0)
-            stage = stage_pool.tile([P, nj, width], F32, name="stage")
-            accs = {}
+            acc = psum.tile([P, j1 - j0, N_TILE], F32, name="acc")
+            if pass_zero_first:
+                order = [(j, 0) for j in range(j0, j1)] + [(j, g) for j in range(j0, j1) for g in range(1, PASSES)]
+            else:
+                order = [(j, g) for j in range(j0, j1) for g in range(PASSES)]
             for j, g in order:
                 m = SEQ_TILES * b + j
-                if g == 0:
-                    acc = psum.tile([P, width], F32, name="acc")
-                    accs[j] = acc
                 cc, cm = chunk_of(X_CODE_CHUNKS, m)
                 pc, pm = chunk_of(X_PLANE_CHUNKS, m)
                 nc.tensor.matmul_mx(
-                    out=accs[j][:],
+                    out=acc[:, j - j0, 0:width],
                     lhsT=x_codes[cc][:, g, 2 * P * cm : 2 * P * (cm + 1)].bitcast(FP4X4),
                     lhsT_scale=x_planes[pc][:, g, P * pm : P * (pm + 1)],
                     rhs=w_operand(n, g)[:, 2 * HEAD_DIM * s0 : 2 * HEAD_DIM * s1].bitcast(FP4X4),
@@ -199,15 +201,22 @@ def tile_pgtattention_pa_kernel(
                     start=(g == 0),
                     stop=(g == PASSES - 1),
                 )
-                if g == PASSES - 1:
-                    nc.vector.tensor_tensor(
-                        out=stage[:, j - j0, :],
-                        in0=accs[j][:],
-                        in1=bias[n][:, HEAD_DIM * s0 : HEAD_DIM * s1],
-                        op=ALU.add,
-                    )
-                    if n == 0 and m + 1 < COL_BLOCKS:
-                        load_w_block(m + 1)
+            for j in reversed(range(j0, j1)):
+                nc.vector.tensor_tensor(
+                    out=stage[:, j - first_j, :],
+                    in0=acc[:, j - j0, 0:width],
+                    in1=bias[n][:, HEAD_DIM * s0 : HEAD_DIM * s1],
+                    op=ALU.add,
+                )
+                if blocks_loaded[0] < COL_BLOCKS:
+                    load_w_block(blocks_loaded[0])
+                    blocks_loaded[0] += 1
+
+        def group(n, b, j0, j1, s0, s1):
+            nj = j1 - j0
+            stage = stage_pool.tile([P, nj, HEAD_DIM * (s1 - s0)], F32, name="stage")
+            for u0 in range(j0, j1, UNIT):
+                unit(n, b, u0, min(u0 + UNIT, j1), s0, s1, stage, j0, n == 0 and b == 0 and u0 == 0)
 
             pieces = [2 * n + s for s in range(s0, s1)]
             rot = [k for k in range(s1 - s0) if pieces[k] % 3 != 2]
@@ -217,42 +226,34 @@ def tile_pgtattention_pa_kernel(
                 nr = r1 - r0
                 straight = rope_pool.tile([P, nj, nr, ROT], F32, name="straight")
                 crossed = rope_pool.tile([P, nj, nr, ROT], F32, name="crossed")
-                nc.vector.tensor_tensor(
+                nc.gpsimd.tensor_tensor(
                     out=straight[:], in0=view[:, :, r0:r1, 0:ROT], in1=cos_v[:, j0:j1, 0:nr, :], op=ALU.mult
                 )
-                nc.vector.tensor_tensor(
+                nc.gpsimd.tensor_tensor(
                     out=crossed[:, :, :, 0:HALF],
                     in0=view[:, :, r0:r1, HALF:ROT],
                     in1=sin_v[:, j0:j1, 0:nr, 0, :],
                     op=ALU.mult,
                 )
-                nc.vector.tensor_tensor(
+                nc.gpsimd.tensor_tensor(
                     out=crossed[:, :, :, HALF:ROT],
                     in0=view[:, :, r0:r1, 0:HALF],
                     in1=sin_v[:, j0:j1, 0:nr, 1, :],
                     op=ALU.mult,
                 )
-                nc.vector.tensor_tensor(
+                nc.gpsimd.tensor_tensor(
                     out=view[:, :, r0:r1, 0:ROT], in0=straight[:], in1=crossed[:], op=ALU.add
                 )
-            for k, q in enumerate(pieces):
+            for k, q in sorted(enumerate(pieces), key=lambda kq: kq[1] % 3 != 2):
                 dst = outs[q % 3][b, q // 3, P * j0 : P * j1, :]
                 nc.scalar.dma_start(out=dst.rearrange("(j p) f -> p j f", p=P), in_=view[:, :, k, :])
 
-        def tile_by_tile(j0, j1):
-            return [(j, g) for j in range(j0, j1) for g in range(PASSES)]
-
-        for n in range(COL_BLOCKS):
+        last = COL_BLOCKS - 1
+        for n in range(last):
             for b in range(BATCH):
-                if n == 0 and b == 0:
-                    order = [(j, 0) for j in range(HEAD_TILES)]
-                    order += [(j, g) for j in range(HEAD_TILES) for g in range(1, PASSES)]
-                    order += tile_by_tile(HEAD_TILES, SEQ_TILES)
-                    group(n, b, 0, SEQ_TILES, 0, 2, order)
-                elif n == COL_BLOCKS - 1:
-                    group(n, b, 0, SEQ_TILES, 0, 1, tile_by_tile(0, SEQ_TILES))
-                else:
-                    group(n, b, 0, SEQ_TILES, 0, 2, tile_by_tile(0, SEQ_TILES))
-        group(COL_BLOCKS - 1, 0, 0, SEQ_TILES, 1, 2, tile_by_tile(0, SEQ_TILES))
+                group(n, b, 0, SEQ_TILES, 0, 2)
+        group(last, 0, 0, SEQ_TILES, 0, 1)
+        group(last, 1, 0, SEQ_TILES, 0, 1)
+        group(last, 0, 0, SEQ_TILES, 1, 2)
         for j0, j1 in ((0, 3), (3, 5), (5, 6)):
-            group(COL_BLOCKS - 1, 1, j0, j1, 1, 2, tile_by_tile(j0, j1))
+            group(last, 1, j0, j1, 1, 2)

@@ -39,9 +39,21 @@ def load_scale_rows(nc, plane, scales, cols):
 
 def load_codes(nc, codes, words, passes, byte_cols):
     nc.sync.dma_start(
-        out=codes[:].bitcast(I32),
+        out=codes.bitcast(I32),
         in_=words[passes, :, byte_cols].rearrange("g p c -> p g c").bitcast(I32),
     )
+
+
+def block_pieces(n):
+    if n < HEADS:
+        return ((0, n), (1, n))
+    return ((2, 2 * (n - HEADS)), (2, 2 * (n - HEADS) + 1))
+
+
+def block_runs(n):
+    if n < HEADS:
+        return ((0, 2, 3 * HEAD_DIM * n),)
+    return tuple([(s, 1, 3 * HEAD_DIM * head + 2 * HEAD_DIM) for s, (part, head) in enumerate(block_pieces(n))])
 
 
 def chunk_of(chunks, m):
@@ -60,8 +72,9 @@ def tile_pgtattention_pa_kernel(
     with ExitStack() as ctx:
         keep = ctx.enter_context(tc.tile_pool(name="keep", bufs=1))
         stage_pool = ctx.enter_context(tc.tile_pool(name="stage", bufs=6))
+        tail_pool = ctx.enter_context(tc.tile_pool(name="tail", bufs=SEQ_TILES + 1))
         rope_pool = ctx.enter_context(tc.tile_pool(name="rope", bufs=2))
-        psum = ctx.enter_context(tc.psum_pool(name="psum", bufs=2))
+        psum = ctx.enter_context(tc.psum_pool(name="psum", bufs=7))
         idle_psum = ctx.enter_context(tc.psum_pool(name="idle_psum", bufs=1))
         ctx.enter_context(tc.manual_schedule())
 
@@ -75,31 +88,51 @@ def tile_pgtattention_pa_kernel(
                 w_codes.append(keep.tile([P, PASSES, 2 * N_TILE], U8, name="w_codes%d" % n, align_bytes=64))
             w_planes.append(keep.tile([P, PASSES, N_TILE], U8, name="w_plane%d" % n, align_bytes=64))
             bias.append(keep.tile([P, N_TILE], BF16, name="bias%d" % n))
-        x_codes = []
+        x_first = keep.tile([P, 1, 2 * P * X_CODE_CHUNKS[0][1]], U8, name="x_first", align_bytes=64)
+        x_rest = keep.tile([P, PASSES - 1, 2 * P * X_CODE_CHUNKS[0][1]], U8, name="x_rest", align_bytes=64)
+        x_codes = [None]
         for c, (m0, m1) in enumerate(X_CODE_CHUNKS):
-            x_codes.append(keep.tile([P, PASSES, 2 * P * (m1 - m0)], U8, name="x_codes%d" % c, align_bytes=64))
+            if c > 0:
+                x_codes.append(keep.tile([P, PASSES, 2 * P * (m1 - m0)], U8, name="x_codes%d" % c, align_bytes=64))
         x_planes = []
         for c, (m0, m1) in enumerate(X_PLANE_CHUNKS):
             x_planes.append(keep.tile([P, PASSES, P * (m1 - m0)], U8, name="x_plane%d" % c, align_bytes=64))
 
-        def w_cols(n):
-            return slice(N_TILE * n, N_TILE * (n + 1))
-
-        def w_byte_cols(n):
-            return slice(2 * N_TILE * n, 2 * N_TILE * (n + 1))
-
         def load_bias(n):
-            nc.gpsimd.dma_start(out=bias[n][:], in_=b_qkv[w_cols(n)].partition_broadcast(P))
+            for s, pieces, col in block_runs(n):
+                nc.gpsimd.dma_start(
+                    out=bias[n][:, HEAD_DIM * s : HEAD_DIM * (s + pieces)],
+                    in_=b_qkv[col : col + HEAD_DIM * pieces].partition_broadcast(P),
+                )
+
+        def load_w_plane(n):
+            for s, pieces, col in block_runs(n):
+                load_scale_rows(
+                    nc,
+                    w_planes[n][:, :, HEAD_DIM * s : HEAD_DIM * (s + pieces)],
+                    W_qkv_scales,
+                    slice(col, col + HEAD_DIM * pieces),
+                )
+
+        def load_w_codes(n, codes, passes):
+            for s, pieces, col in block_runs(n):
+                load_codes(
+                    nc,
+                    codes[:, :, 2 * HEAD_DIM * s : 2 * HEAD_DIM * (s + pieces)],
+                    W_qkv_words,
+                    passes,
+                    slice(2 * col, 2 * (col + HEAD_DIM * pieces)),
+                )
 
         def load_w_block(n):
             nc.gpsimd.memset(w_planes[n][:].bitcast(F32), 0.0)
-            load_scale_rows(nc, w_planes[n], W_qkv_scales, w_cols(n))
-            load_codes(nc, w_codes[n], W_qkv_words, slice(0, PASSES), w_byte_cols(n))
+            load_w_plane(n)
+            load_w_codes(n, w_codes[n], slice(0, PASSES))
             load_bias(n)
 
         def load_x_codes(c):
             m0, m1 = X_CODE_CHUNKS[c]
-            load_codes(nc, x_codes[c], hidden_states_words, slice(0, PASSES), slice(2 * P * m0, 2 * P * m1))
+            load_codes(nc, x_codes[c][:], hidden_states_words, slice(0, PASSES), slice(2 * P * m0, 2 * P * m1))
 
         def load_x_plane(c):
             m0, m1 = X_PLANE_CHUNKS[c]
@@ -113,11 +146,13 @@ def tile_pgtattention_pa_kernel(
         nc.gpsimd.memset(w_planes[0][:].bitcast(F32), 0.0)
         nc.gpsimd.memset(x_planes[0][:].bitcast(F32), 0.0)
         nc.vector.memset(x_planes[1][:].bitcast(I32), 0)
-        load_codes(nc, w_first, W_qkv_words, slice(0, 1), w_byte_cols(0))
-        load_x_codes(0)
-        load_scale_rows(nc, w_planes[0], W_qkv_scales, w_cols(0))
+        first_x_bytes = slice(0, 2 * P * X_CODE_CHUNKS[0][1])
+        load_w_codes(0, w_first, slice(0, 1))
+        load_codes(nc, x_first[:], hidden_states_words, slice(0, 1), first_x_bytes)
+        load_w_plane(0)
         load_x_plane(0)
-        load_codes(nc, w_rest, W_qkv_words, slice(1, PASSES), w_byte_cols(0))
+        load_w_codes(0, w_rest, slice(1, PASSES))
+        load_codes(nc, x_rest[:], hidden_states_words, slice(1, PASSES), first_x_bytes)
         load_x_plane(1)
         load_x_codes(1)
         load_x_codes(2)
@@ -179,11 +214,16 @@ def tile_pgtattention_pa_kernel(
                 return w_codes[n][:, g, :]
             return w_first[:, 0, :] if g == 0 else w_rest[:, g - 1, :]
 
+        def x_operand(c, g):
+            if c > 0:
+                return x_codes[c][:, g, :]
+            return x_first[:, 0, :] if g == 0 else x_rest[:, g - 1, :]
+
         blocks_loaded = [1]
 
         def unit(n, b, j0, j1, s0, s1, stage, first_j, pass_zero_first):
             width = HEAD_DIM * (s1 - s0)
-            acc = psum.tile([P, j1 - j0, N_TILE], F32, name="acc")
+            acc = [psum.tile([P, N_TILE], F32, name="acc") for j in range(j0, j1)]
             if pass_zero_first:
                 order = [(j, 0) for j in range(j0, j1)] + [(j, g) for j in range(j0, j1) for g in range(1, PASSES)]
             else:
@@ -193,8 +233,8 @@ def tile_pgtattention_pa_kernel(
                 cc, cm = chunk_of(X_CODE_CHUNKS, m)
                 pc, pm = chunk_of(X_PLANE_CHUNKS, m)
                 nc.tensor.matmul_mx(
-                    out=acc[:, j - j0, 0:width],
-                    lhsT=x_codes[cc][:, g, 2 * P * cm : 2 * P * (cm + 1)].bitcast(FP4X4),
+                    out=acc[j - j0][:, 0:width],
+                    lhsT=x_operand(cc, g)[:, 2 * P * cm : 2 * P * (cm + 1)].bitcast(FP4X4),
                     lhsT_scale=x_planes[pc][:, g, P * pm : P * (pm + 1)],
                     rhs=w_operand(n, g)[:, 2 * HEAD_DIM * s0 : 2 * HEAD_DIM * s1].bitcast(FP4X4),
                     rhs_scale=w_planes[n][:, g, HEAD_DIM * s0 : HEAD_DIM * s1],
@@ -204,7 +244,7 @@ def tile_pgtattention_pa_kernel(
             for j in reversed(range(j0, j1)):
                 nc.vector.tensor_tensor(
                     out=stage[:, j - first_j, :],
-                    in0=acc[:, j - j0, 0:width],
+                    in0=acc[j - j0][:, 0:width],
                     in1=bias[n][:, HEAD_DIM * s0 : HEAD_DIM * s1],
                     op=ALU.add,
                 )
@@ -214,12 +254,15 @@ def tile_pgtattention_pa_kernel(
 
         def group(n, b, j0, j1, s0, s1):
             nj = j1 - j0
-            stage = stage_pool.tile([P, nj, HEAD_DIM * (s1 - s0)], F32, name="stage")
+            if nj > 1:
+                stage = stage_pool.tile([P, nj, HEAD_DIM * (s1 - s0)], F32, name="stage")
+            else:
+                stage = tail_pool.tile([P, nj, HEAD_DIM * (s1 - s0)], F32, name="tail_stage")
             for u0 in range(j0, j1, UNIT):
                 unit(n, b, u0, min(u0 + UNIT, j1), s0, s1, stage, j0, n == 0 and b == 0 and u0 == 0)
 
-            pieces = [2 * n + s for s in range(s0, s1)]
-            rot = [k for k in range(s1 - s0) if pieces[k] % 3 != 2]
+            pieces = block_pieces(n)[s0:s1]
+            rot = [k for k in range(s1 - s0) if pieces[k][0] != 2]
             view = stage[:].rearrange("p j (s f) -> p j s f", f=HEAD_DIM)
             if rot:
                 r0, r1 = rot[0], rot[-1] + 1
@@ -244,16 +287,17 @@ def tile_pgtattention_pa_kernel(
                 nc.gpsimd.tensor_tensor(
                     out=view[:, :, r0:r1, 0:ROT], in0=straight[:], in1=crossed[:], op=ALU.add
                 )
-            for k, q in sorted(enumerate(pieces), key=lambda kq: kq[1] % 3 != 2):
-                dst = outs[q % 3][b, q // 3, P * j0 : P * j1, :]
+            for k, (part, head) in enumerate(pieces):
+                dst = outs[part][b, head, P * j0 : P * j1, :]
                 nc.scalar.dma_start(out=dst.rearrange("(j p) f -> p j f", p=P), in_=view[:, :, k, :])
 
         last = COL_BLOCKS - 1
         for n in range(last):
             for b in range(BATCH):
                 group(n, b, 0, SEQ_TILES, 0, 2)
-        group(last, 0, 0, SEQ_TILES, 0, 1)
-        group(last, 1, 0, SEQ_TILES, 0, 1)
-        group(last, 0, 0, SEQ_TILES, 1, 2)
-        for j0, j1 in ((0, 3), (3, 5), (5, 6)):
-            group(last, 1, j0, j1, 1, 2)
+        group(last, 0, 0, 3, 0, 2)
+        group(last, 0, 3, SEQ_TILES, 0, 2)
+        for j in range(SEQ_TILES - 1):
+            group(last, 1, j, j + 1, 0, 2)
+        group(last, 1, 5, 6, 0, 1)
+        group(last, 1, 5, 6, 1, 2)

@@ -244,8 +244,8 @@ def tile_pgtattention_pa_kernel(
             for j in reversed(range(j0, j1)):
                 nc.vector.tensor_tensor(
                     out=stage[:, j - first_j, :],
-                    in0=acc[j - j0][:, 0:width],
-                    in1=bias[n][:, HEAD_DIM * s0 : HEAD_DIM * s1],
+                    in0=bias[n][:, HEAD_DIM * s0 : HEAD_DIM * s1],
+                    in1=acc[j - j0][:, 0:width],
                     op=ALU.add,
                 )
                 if blocks_loaded[0] < COL_BLOCKS:

@@ -100,7 +100,7 @@ def tile_pgtattention_pa_kernel(
 
         def load_bias(n):
             for s, pieces, col in block_runs(n):
-                nc.gpsimd.dma_start(
+                nc.sync.dma_start(
                     out=bias[n][:, HEAD_DIM * s : HEAD_DIM * (s + pieces)],
                     in_=b_qkv[col : col + HEAD_DIM * pieces].partition_broadcast(P),
                 )
@@ -156,9 +156,9 @@ def tile_pgtattention_pa_kernel(
         load_x_plane(1)
         load_x_codes(1)
         load_x_codes(2)
+        load_bias(0)
         pos_i = keep.tile([P, SEQ_TILES], I32, name="pos_i")
         nc.gpsimd.iota(pos_i[:], pattern=[[P, SEQ_TILES]], base=0, channel_multiplier=1)
-        load_bias(0)
 
         pos = keep.tile([P, SEQ_TILES], F32, name="pos")
         nc.vector.tensor_copy(out=pos[:], in_=pos_i[:])

@@ -22,7 +22,8 @@ TOKEN_TILES = BATCH * SEQ_TILES
 HALF = ROT // 2
 X_CODE_CHUNKS = ((0, 3), (3, 6), (6, 12))
 X_PLANE_CHUNKS = ((0, 3), (3, 12))
-UNIT = 3
+UNIT = 6
+FIRST = 3
 WARM_UP = 10
 SIN_LIMIT = 0.5 - 1e-6
 
@@ -74,8 +75,7 @@ def tile_pgtattention_pa_kernel(
         stage_pool = ctx.enter_context(tc.tile_pool(name="stage", bufs=6))
         tail_pool = ctx.enter_context(tc.tile_pool(name="tail", bufs=SEQ_TILES + 1))
         rope_pool = ctx.enter_context(tc.tile_pool(name="rope", bufs=2))
-        psum = ctx.enter_context(tc.psum_pool(name="psum", bufs=7))
-        idle_psum = ctx.enter_context(tc.psum_pool(name="idle_psum", bufs=1))
+        psum = ctx.enter_context(tc.psum_pool(name="psum", bufs=8))
         ctx.enter_context(tc.manual_schedule())
 
         w_first = keep.tile([P, 1, 2 * N_TILE], U8, name="w_first", align_bytes=64)
@@ -140,7 +140,7 @@ def tile_pgtattention_pa_kernel(
 
         idle = keep.tile([P, N_TILE], BF16, name="idle")
         nc.vector.memset(idle[:], 0.0)
-        idle_acc = idle_psum.tile([P, N_TILE], F32, name="idle_acc")
+        idle_acc = psum.tile([P, N_TILE], F32, name="acc")
         for i in range(WARM_UP):
             nc.tensor.matmul(out=idle_acc[:], lhsT=idle[:, 0:P], rhs=idle[:], start=True, stop=True)
         nc.gpsimd.memset(w_planes[0][:].bitcast(F32), 0.0)
@@ -225,7 +225,8 @@ def tile_pgtattention_pa_kernel(
             width = HEAD_DIM * (s1 - s0)
             acc = [psum.tile([P, N_TILE], F32, name="acc") for j in range(j0, j1)]
             if pass_zero_first:
-                order = [(j, 0) for j in range(j0, j1)] + [(j, g) for j in range(j0, j1) for g in range(1, PASSES)]
+                order = [(j, 0) for j in range(FIRST)] + [(j, g) for j in range(FIRST) for g in range(1, PASSES)]
+                order += [(j, g) for j in range(FIRST, j1) for g in range(PASSES)]
             else:
                 order = [(j, g) for j in range(j0, j1) for g in range(PASSES)]
             for j, g in order:
@@ -241,7 +242,7 @@ def tile_pgtattention_pa_kernel(
                     start=(g == 0),
                     stop=(g == PASSES - 1),
                 )
-            for j in reversed(range(j0, j1)):
+            for j in list(range(j0 + 1, j1)) + [j0]:
                 nc.vector.tensor_tensor(
                     out=stage[:, j - first_j, :],
                     in0=bias[n][:, HEAD_DIM * s0 : HEAD_DIM * s1],

@@ -288,9 +288,14 @@ def tile_pgtattention_pa_kernel(
                 nc.gpsimd.tensor_tensor(
                     out=view[:, :, r0:r1, 0:ROT], in0=straight[:], in1=crossed[:], op=ALU.add
                 )
-            for k, (part, head) in enumerate(pieces):
-                dst = outs[part][b, head, P * j0 : P * j1, :]
-                nc.scalar.dma_start(out=dst.rearrange("(j p) f -> p j f", p=P), in_=view[:, :, k, :])
+            if nj == 1 and len(pieces) == 2 and not rot:
+                head = pieces[0][1]
+                dst = outs[2][b, head : head + 2, P * j0 : P * j1, :]
+                nc.scalar.dma_start(out=dst.rearrange("h p f -> p h f"), in_=view[:, 0, :, :])
+            else:
+                for k, (part, head) in enumerate(pieces):
+                    dst = outs[part][b, head, P * j0 : P * j1, :]
+                    nc.scalar.dma_start(out=dst.rearrange("(j p) f -> p j f", p=P), in_=view[:, :, k, :])
 
         last = COL_BLOCKS - 1
         for n in range(last):

import math
from contextlib import ExitStack

import concourse.mybir as mybir

F32 = mybir.dt.float32
BF16 = mybir.dt.bfloat16
I32 = mybir.dt.int32
U8 = mybir.dt.uint8
FP4X4 = mybir.dt.float4_e2m1fn_x4
ALU = mybir.AluOpType
ACT = mybir.ActivationFunctionType

BATCH, SEQ, HIDDEN, HEADS, HEAD_DIM, ROT = 2, 768, 2048, 8, 256, 32
BASE = 10000.0
P = 128
PASSES = HIDDEN // 512
N_TILE = 512
COL_BLOCKS = 3 * HIDDEN // N_TILE
SEQ_TILES = SEQ // P
TOKEN_TILES = BATCH * SEQ_TILES
HALF = ROT // 2
X_CODE_CHUNKS = ((0, 3), (3, 6), (6, 12))
X_PLANE_CHUNKS = ((0, 3), (3, 12))
UNIT = 6
FIRST = 3
WARM_UP = 10
SIN_LIMIT = 0.5 - 1e-6

FLOPS = 2 * BATCH * SEQ * HIDDEN * 3 * HIDDEN


def load_scale_rows(nc, plane, scales, cols):
    for quad in range(4):
        nc.sync.dma_start(
            out=plane[32 * quad : 32 * quad + 4, :, :].bitcast(I32),
            in_=scales[:, 4 * quad : 4 * quad + 4, cols].rearrange("g r n -> r g n").bitcast(I32),
        )


def load_codes(nc, codes, words, passes, byte_cols):
    nc.sync.dma_start(
        out=codes.bitcast(I32),
        in_=words[passes, :, byte_cols].rearrange("g p c -> p g c").bitcast(I32),
    )


def block_pieces(n):
    if n < HEADS:
        return ((0, n), (1, n))
    return ((2, 2 * (n - HEADS)), (2, 2 * (n - HEADS) + 1))


def block_runs(n):
    if n < HEADS:
        return ((0, 2, 3 * HEAD_DIM * n),)
    return tuple([(s, 1, 3 * HEAD_DIM * head + 2 * HEAD_DIM) for s, (part, head) in enumerate(block_pieces(n))])


def chunk_of(chunks, m):
    for c, (m0, m1) in enumerate(chunks):
        if m0 <= m < m1:
            return c, m - m0
    raise ValueError("no such token tile")


def tile_pgtattention_pa_kernel(
    tc, hidden_states_words, hidden_states_scales, W_qkv_words, W_qkv_scales, b_qkv, out_0, out_1, out_2
):
    nc = tc.nc
    outs = (out_0, out_1, out_2)

    with ExitStack() as ctx:
        keep = ctx.enter_context(tc.tile_pool(name="keep", bufs=1))
        stage_pool = ctx.enter_context(tc.tile_pool(name="stage", bufs=6))
        tail_pool = ctx.enter_context(tc.tile_pool(name="tail", bufs=SEQ_TILES + 1))
        rope_pool = ctx.enter_context(tc.tile_pool(name="rope", bufs=2))
        psum = ctx.enter_context(tc.psum_pool(name="psum", bufs=8))
        ctx.enter_context(tc.manual_schedule())

        w_first = keep.tile([P, 1, 2 * N_TILE], U8, name="w_first", align_bytes=64)
        w_rest = keep.tile([P, PASSES - 1, 2 * N_TILE], U8, name="w_rest", align_bytes=64)
        w_codes = [None]
        w_planes = []
        bias = []
        for n in range(COL_BLOCKS):
            if n > 0:
                w_codes.append(keep.tile([P, PASSES, 2 * N_TILE], U8, name="w_codes%d" % n, align_bytes=64))
            w_planes.append(keep.tile([P, PASSES, N_TILE], U8, name="w_plane%d" % n, align_bytes=64))
            bias.append(keep.tile([P, N_TILE], BF16, name="bias%d" % n))
        x_first = keep.tile([P, 1, 2 * P * X_CODE_CHUNKS[0][1]], U8, name="x_first", align_bytes=64)
        x_rest = keep.tile([P, PASSES - 1, 2 * P * X_CODE_CHUNKS[0][1]], U8, name="x_rest", align_bytes=64)
        x_codes = [None]
        for c, (m0, m1) in enumerate(X_CODE_CHUNKS):
            if c > 0:
                x_codes.append(keep.tile([P, PASSES, 2 * P * (m1 - m0)], U8, name="x_codes%d" % c, align_bytes=64))
        x_planes = []
        for c, (m0, m1) in enumerate(X_PLANE_CHUNKS):
            x_planes.append(keep.tile([P, PASSES, P * (m1 - m0)], U8, name="x_plane%d" % c, align_bytes=64))

        def load_bias(n):
            for s, pieces, col in block_runs(n):
                nc.sync.dma_start(
                    out=bias[n][:, HEAD_DIM * s : HEAD_DIM * (s + pieces)],
                    in_=b_qkv[col : col + HEAD_DIM * pieces].partition_broadcast(P),
                )

        def load_w_plane(n):
            for s, pieces, col in block_runs(n):
                load_scale_rows(
                    nc,
                    w_planes[n][:, :, HEAD_DIM * s : HEAD_DIM * (s + pieces)],
                    W_qkv_scales,
                    slice(col, col + HEAD_DIM * pieces),
                )

        def load_w_codes(n, codes, passes):
            for s, pieces, col in block_runs(n):
                load_codes(
                    nc,
                    codes[:, :, 2 * HEAD_DIM * s : 2 * HEAD_DIM * (s + pieces)],
                    W_qkv_words,
                    passes,
                    slice(2 * col, 2 * (col + HEAD_DIM * pieces)),
                )

        def load_w_block(n):
            nc.gpsimd.memset(w_planes[n][:].bitcast(F32), 0.0)
            load_w_plane(n)
            load_w_codes(n, w_codes[n], slice(0, PASSES))
            load_bias(n)

        def load_x_codes(c):
            m0, m1 = X_CODE_CHUNKS[c]
            load_codes(nc, x_codes[c][:], hidden_states_words, slice(0, PASSES), slice(2 * P * m0, 2 * P * m1))

        def load_x_plane(c):
            m0, m1 = X_PLANE_CHUNKS[c]
            load_scale_rows(nc, x_planes[c], hidden_states_scales, slice(P * m0, P * m1))

        idle = keep.tile([P, N_TILE], BF16, name="idle")
        nc.vector.memset(idle[:], 0.0)
        idle_acc = psum.tile([P, N_TILE], F32, name="acc")
        for i in range(WARM_UP):
            nc.tensor.matmul(out=idle_acc[:], lhsT=idle[:, 0:P], rhs=idle[:], start=True, stop=True)
        nc.gpsimd.memset(w_planes[0][:].bitcast(F32), 0.0)
        nc.gpsimd.memset(x_planes[0][:].bitcast(F32), 0.0)
        nc.vector.memset(x_planes[1][:].bitcast(I32), 0)
        first_x_bytes = slice(0, 2 * P * X_CODE_CHUNKS[0][1])
        load_w_codes(0, w_first, slice(0, 1))
        load_codes(nc, x_first[:], hidden_states_words, slice(0, 1), first_x_bytes)
        load_w_plane(0)
        load_x_plane(0)
        load_w_codes(0, w_rest, slice(1, PASSES))
        load_codes(nc, x_rest[:], hidden_states_words, slice(1, PASSES), first_x_bytes)
        load_x_plane(1)
        load_x_codes(1)
        load_x_codes(2)
        load_bias(0)
        pos_i = keep.tile([P, SEQ_TILES], I32, name="pos_i")
        nc.gpsimd.iota(pos_i[:], pattern=[[P, SEQ_TILES]], base=0, channel_multiplier=1)

        pos = keep.tile([P, SEQ_TILES], F32, name="pos")
        nc.vector.tensor_copy(out=pos[:], in_=pos_i[:])
        turns = keep.tile([P, SEQ_TILES, 2, HALF], F32, name="turns")
        for i in range(HALF):
            nc.vector.tensor_scalar(
                out=turns[:, :, :, i],
                in0=pos[:].unsqueeze(2).to_broadcast([P, SEQ_TILES, 2]),
                scalar1=1.0 / (BASE ** (i / HALF)) / (2.0 * math.pi),
                scalar2=None,
                op0=ALU.mult,
            )
        nc.vector.tensor_scalar(
            out=turns[:, :, 0, :], in0=turns[:, :, 0, :], scalar1=0.25, scalar2=None, op0=ALU.add
        )
        whole_i = keep.tile([P, SEQ_TILES, 2, HALF], I32, name="whole_i")
        nc.vector.tensor_copy(out=whole_i[:], in_=turns[:])
        whole = keep.tile([P, SEQ_TILES, 2, HALF], F32, name="whole")
        nc.vector.tensor_copy(out=whole[:], in_=whole_i[:])
        frac = keep.tile([P, SEQ_TILES, 2, HALF], F32, name="frac")
        nc.vector.tensor_tensor(out=frac[:], in0=turns[:], in1=whole[:], op=ALU.subtract)
        over = keep.tile([P, SEQ_TILES, 2, HALF], F32, name="over")
        nc.vector.tensor_scalar(out=over[:], in0=frac[:], scalar1=0.5, scalar2=None, op0=ALU.is_gt)
        wrapped = keep.tile([P, SEQ_TILES, 2, HALF], F32, name="wrapped")
        nc.vector.tensor_tensor(out=wrapped[:], in0=frac[:], in1=over[:], op=ALU.subtract)
        clamped = keep.tile([P, SEQ_TILES, 2, HALF], F32, name="clamped")
        nc.vector.tensor_scalar(
            out=clamped[:], in0=wrapped[:], scalar1=-SIN_LIMIT, scalar2=SIN_LIMIT, op0=ALU.max, op1=ALU.min
        )
        cos_sin = keep.tile([P, SEQ_TILES, 2, HALF], F32, name="cos_sin")
        nc.scalar.activation(out=cos_sin[:], in_=clamped[:], func=ACT.Sin, scale=2.0 * math.pi)
        cos_t = keep.tile([P, SEQ_TILES, 4, HALF], F32, name="cos_t")
        nc.vector.tensor_copy(
            out=cos_t[:], in_=cos_sin[:, :, 0, :].unsqueeze(2).to_broadcast([P, SEQ_TILES, 4, HALF])
        )
        sin_t = keep.tile([P, SEQ_TILES, 2, 2, HALF], F32, name="sin_t")
        nc.vector.tensor_scalar(
            out=sin_t[:, :, :, 0, :],
            in0=cos_sin[:, :, 1, :].unsqueeze(2).to_broadcast([P, SEQ_TILES, 2, HALF]),
            scalar1=-1.0,
            scalar2=None,
            op0=ALU.mult,
        )
        nc.vector.tensor_copy(
            out=sin_t[:, :, :, 1, :],
            in_=cos_sin[:, :, 1, :].unsqueeze(2).to_broadcast([P, SEQ_TILES, 2, HALF]),
        )
        cos_v = cos_t[:].rearrange("p j (s r) i -> p j s (r i)", s=2)
        sin_v = sin_t[:]

        def w_operand(n, g):
            if n > 0:
                return w_codes[n][:, g, :]
            return w_first[:, 0, :] if g == 0 else w_rest[:, g - 1, :]

        def x_operand(c, g):
            if c > 0:
                return x_codes[c][:, g, :]
            return x_first[:, 0, :] if g == 0 else x_rest[:, g - 1, :]

        blocks_loaded = [1]

        def unit(n, b, j0, j1, s0, s1, stage, first_j, pass_zero_first):
            width = HEAD_DIM * (s1 - s0)
            acc = [psum.tile([P, N_TILE], F32, name="acc") for j in range(j0, j1)]
            if pass_zero_first:
                order = [(j, 0) for j in range(FIRST)] + [(j, g) for j in range(FIRST) for g in range(1, PASSES)]
                order += [(j, g) for j in range(FIRST, j1) for g in range(PASSES)]
            else:
                order = [(j, g) for j in range(j0, j1) for g in range(PASSES)]
            for j, g in order:
                m = SEQ_TILES * b + j
                cc, cm = chunk_of(X_CODE_CHUNKS, m)
                pc, pm = chunk_of(X_PLANE_CHUNKS, m)
                nc.tensor.matmul_mx(
                    out=acc[j - j0][:, 0:width],
                    lhsT=x_operand(cc, g)[:, 2 * P * cm : 2 * P * (cm + 1)].bitcast(FP4X4),
                    lhsT_scale=x_planes[pc][:, g, P * pm : P * (pm + 1)],
                    rhs=w_operand(n, g)[:, 2 * HEAD_DIM * s0 : 2 * HEAD_DIM * s1].bitcast(FP4X4),
                    rhs_scale=w_planes[n][:, g, HEAD_DIM * s0 : HEAD_DIM * s1],
                    start=(g == 0),
                    stop=(g == PASSES - 1),
                )
            for j in list(range(j0 + 1, j1)) + [j0]:
                nc.vector.tensor_tensor(
                    out=stage[:, j - first_j, :],
                    in0=bias[n][:, HEAD_DIM * s0 : HEAD_DIM * s1],
                    in1=acc[j - j0][:, 0:width],
                    op=ALU.add,
                )
                if blocks_loaded[0] < COL_BLOCKS:
                    load_w_block(blocks_loaded[0])
                    blocks_loaded[0] += 1

        def group(n, b, j0, j1, s0, s1):
            nj = j1 - j0
            if nj > 1:
                stage = stage_pool.tile([P, nj, HEAD_DIM * (s1 - s0)], F32, name="stage")
            else:
                stage = tail_pool.tile([P, nj, HEAD_DIM * (s1 - s0)], F32, name="tail_stage")
            for u0 in range(j0, j1, UNIT):
                unit(n, b, u0, min(u0 + UNIT, j1), s0, s1, stage, j0, n == 0 and b == 0 and u0 == 0)

            pieces = block_pieces(n)[s0:s1]
            rot = [k for k in range(s1 - s0) if pieces[k][0] != 2]
            view = stage[:].rearrange("p j (s f) -> p j s f", f=HEAD_DIM)
            if rot:
                r0, r1 = rot[0], rot[-1] + 1
                nr = r1 - r0
                straight = rope_pool.tile([P, nj, nr, ROT], F32, name="straight")
                crossed = rope_pool.tile([P, nj, nr, ROT], F32, name="crossed")
                nc.gpsimd.tensor_tensor(
                    out=straight[:], in0=view[:, :, r0:r1, 0:ROT], in1=cos_v[:, j0:j1, 0:nr, :], op=ALU.mult
                )
                nc.gpsimd.tensor_tensor(
                    out=crossed[:, :, :, 0:HALF],
                    in0=view[:, :, r0:r1, HALF:ROT],
                    in1=sin_v[:, j0:j1, 0:nr, 0, :],
                    op=ALU.mult,
                )
                nc.gpsimd.tensor_tensor(
                    out=crossed[:, :, :, HALF:ROT],
                    in0=view[:, :, r0:r1, 0:HALF],
                    in1=sin_v[:, j0:j1, 0:nr, 1, :],
                    op=ALU.mult,
                )
                nc.gpsimd.tensor_tensor(
                    out=view[:, :, r0:r1, 0:ROT], in0=straight[:], in1=crossed[:], op=ALU.add
                )
            if nj == 1 and len(pieces) == 2 and not rot:
                head = pieces[0][1]
                dst = outs[2][b, head : head + 2, P * j0 : P * j1, :]
                nc.scalar.dma_start(out=dst.rearrange("h p f -> p h f"), in_=view[:, 0, :, :])
            else:
                for k, (part, head) in enumerate(pieces):
                    dst = outs[part][b, head, P * j0 : P * j1, :]
                    nc.scalar.dma_start(out=dst.rearrange("(j p) f -> p j f", p=P), in_=view[:, :, k, :])

        last = COL_BLOCKS - 1
        for n in range(last):
            for b in range(BATCH):
                group(n, b, 0, SEQ_TILES, 0, 2)
        group(last, 0, 0, 3, 0, 2)
        group(last, 0, 3, SEQ_TILES, 0, 2)
        for j in range(SEQ_TILES - 1):
            group(last, 1, j, j + 1, 0, 2)
        group(last, 1, 5, 6, 0, 1)
        group(last, 1, 5, 6, 1, 2)
